import numpy as np
import ml_dtypes


def mxq(x, axis, fmt="e4m3"):
    dtype, down = {"e4m3": (ml_dtypes.float8_e4m3fn, 7), "e5m2": (ml_dtypes.float8_e5m2, 14)}[fmt]
    v = np.moveaxis(np.asarray(x, np.float32).astype(ml_dtypes.bfloat16).astype(np.float64), axis, -1)
    blocks = v.reshape(v.shape[:-1] + (-1, 32))
    amax = np.abs(blocks).max(-1, keepdims=True)
    byte = np.maximum(np.where(amax > 0, np.frexp(amax)[1] - 1 + 127, 0) - down, 1)
    scale = np.exp2(byte - 127.0)
    codes = (blocks / scale).astype(np.float32).astype(dtype).astype(np.float64)
    return np.moveaxis((codes * scale).reshape(v.shape), -1, axis)


WIDE = False


def mx_kscale(k):
    if not WIDE:
        return np.ones(k)
    levels = np.array([10, -10, 5, -5, 0])
    a = np.random.permutation(np.resize(levels, k // 512 * 4)).reshape(k // 512, 4)
    idx = np.arange(k)
    return np.exp2(a[idx // 512, idx % 128 // 32])


BF16 = ml_dtypes.bfloat16


def bf(x):
    return np.asarray(x, np.float32).astype(BF16)


def f64(x):
    return np.asarray(x).astype(np.float64)


E2M1 = np.array([0.0, 0.5, 1.0, 1.5, 2.0, 3.0, 4.0, 6.0, -0.0, -0.5, -1.0, -1.5, -2.0, -3.0, -4.0, -6.0])


def pack_weight(w, fmt):
    k, n = w.shape
    w = f64(bf(w)).reshape(k // 32, 32, n)
    amax = np.abs(w).max(1)
    if fmt == "e4m3":
        byte = np.frexp(amax)[1] - 1 + 127 - 7
    else:
        mant, ex = np.frexp(amax / 6.0)
        byte = np.where(mant > 0.5, ex, ex - 1) + 127
    byte = np.clip(np.where(amax > 0, byte, 1), 1, 254)
    scaled = (w * np.exp2(127.0 - byte)[:, None, :]).reshape(k, n).astype(np.float32)
    by_word = np.ascontiguousarray(scaled.reshape(k // 512, 128, 4, n).transpose(0, 1, 3, 2))
    if fmt == "e4m3":
        words = by_word.astype(ml_dtypes.float8_e4m3fn).view(np.uint8)
    else:
        c = by_word.astype(ml_dtypes.float4_e2m1fn).view(np.uint8) & 0xF
        words = c[..., 0::2] | (c[..., 1::2] << 4)
    return np.ascontiguousarray(words), np.ascontiguousarray(byte.astype(np.uint8).reshape(k // 512, 16, n))


def unpack_weight(words, scales, fmt):
    g, p, n, _ = words.shape
    if fmt == "e4m3":
        vals = np.ascontiguousarray(words).view(ml_dtypes.float8_e4m3fn).astype(np.float64)
    else:
        nib = np.empty((g, p, n, 4), np.uint8)
        nib[..., 0::2] = words & 0xF
        nib[..., 1::2] = words >> 4
        vals = E2M1[nib]
    vals = vals * np.repeat(np.exp2(scales.astype(np.float64) - 127.0), 8, axis=1)[..., None]
    return vals.transpose(0, 1, 3, 2).reshape(g * 512, n)

def pack4(w):
    words, scales = pack_weight(w, "e2m1")
    return words.reshape(words.shape[0], 128, -1), scales


def unpack4(words, scales):
    return unpack_weight(words.reshape(words.shape[0], 128, -1, 2), scales, "e2m1")


B, C, H, W, P = 4, 1024, 64, 32, 1024
HP, WP = H // 2, W // 2
M = HP * WP
EPS = 1e-5


def maxpool2x2(x):
    return x.reshape(B, C, HP, 2, WP, 2).max(axis=(3, 5))


def setup_inputs():
    s = mx_kscale(C)
    x = bf(np.random.standard_normal((B, C, H, W)) * s[None, :, None, None])
    wk = np.random.standard_normal((P, C)) / np.sqrt(C) / s[None, :]
    wk_words, wk_scales = pack4(np.ascontiguousarray(wk.T))
    bk = bf(np.random.standard_normal(P) * 0.1)
    wv = np.random.standard_normal((P, C)) / np.sqrt(C) / s[None, :]
    wv_words, wv_scales = pack4(np.ascontiguousarray(wv.T))
    bv = bf(np.random.standard_normal(P) * 0.1)
    return {'x': x,
            'wk_words': wk_words,
            'wk_scales': wk_scales,
            'bk': bk,
            'wv_words': wv_words,
            'wv_scales': wv_scales,
            'bv': bv,
            'k_gamma': bf(np.random.uniform(0.5, 1.5, P)),
            'k_beta': bf(np.random.standard_normal(P) * 0.1),
            'k_mean': bf(np.random.standard_normal(P) * 0.1),
            'k_var': bf(np.random.uniform(0.5, 1.5, P))}


def reference(x, wk_words, wk_scales, bk, wv_words, wv_scales, bv, k_gamma, k_beta, k_mean, k_var):
    xp = mxq(maxpool2x2(f64(x)).reshape(B, C, M), 1, 'e4m3')
    k = (unpack4(wk_words, wk_scales).T @ xp) + f64(bk)[None, :, None]
    sc = f64(k_gamma) / np.sqrt(f64(k_var) + EPS)
    k = (k - f64(k_mean)[None, :, None]) * sc[None, :, None] + f64(k_beta)[None, :, None]
    v = (unpack4(wv_words, wv_scales).T @ xp) + f64(bv)[None, :, None]
    return k.reshape(B, P, HP, WP), v.reshape(B, P, HP, WP)

@@ -1,0 +1,166 @@
+from contextlib import ExitStack
+
+import concourse.mybir as mybir
+from concourse.masks import make_identity
+
+BF16 = mybir.dt.bfloat16
+F32 = mybir.dt.float32
+I32 = mybir.dt.int32
+U32 = mybir.dt.uint32
+U8 = mybir.dt.uint8
+FP8X4 = mybir.dt.float8_e4m3fn_x4
+FP4X4 = mybir.dt.float4_e2m1fn_x4
+IDENTITY = mybir.ActivationFunctionType.Identity
+
+BATCH, CHANNELS, HEIGHT, WIDTH, OUT_CHANNELS = 4, 1024, 64, 32, 1024
+EPS = 1e-5
+PIXELS = (HEIGHT // 2) * (WIDTH // 2)
+
+P = 128
+PACK = 4
+PASSES = CHANNELS // (P * PACK)
+OUT_TILES = OUT_CHANNELS // P
+CONVS = 2
+STORE_TILES = 4
+LIVE_ROWS = 4
+QUADRANTS = 4
+
+FLOPS = 2 * CONVS * BATCH * OUT_CHANNELS * CHANNELS * PIXELS
+
+
+def tile_nonlocalnd_bn_pa_t_kernel(
+    tc, x, wk_words, wk_scales, bk, wv_words, wv_scales, bv, k_gamma, k_beta, k_mean, k_var, out_0, out_1
+):
+    nc = tc.nc
+    words_in = (wk_words, wv_words)
+    scales_in = (wk_scales, wv_scales)
+    outs = (out_0, out_1)
+    x_rows = x.rearrange("b (c p t) h w -> b c p (t h w)", p=P, t=PACK)
+
+    with ExitStack() as stack:
+        stack.enter_context(tc.manual_schedule())
+        const = stack.enter_context(tc.tile_pool(name="const", bufs=1))
+        x_pool = stack.enter_context(tc.tile_pool(name="x", bufs=BATCH * PASSES))
+        work = stack.enter_context(tc.tile_pool(name="work", bufs=2))
+        quant = stack.enter_context(tc.tile_pool(name="quant", bufs=BATCH))
+        stage = stack.enter_context(tc.tile_pool(name="stage", bufs=5))
+        setup_psum = stack.enter_context(tc.psum_pool(name="setup_psum", bufs=1))
+        psum = stack.enter_context(tc.psum_pool(name="psum", bufs=7))
+
+        vectors = (bk, bv, k_gamma, k_beta, k_mean, k_var)
+        BK, BV, GAMMA, BETA, MEAN, VAR = range(6)
+        vector_rows = const.tile([P, P], BF16)
+        nc.vector.memset(vector_rows[:], 0.0)
+        for v, vector in enumerate(vectors):
+            nc.scalar.dma_start(
+                out=vector_rows[OUT_TILES * v : OUT_TILES * (v + 1), :],
+                in_=vector.rearrange("(j p) -> j p", p=P),
+            )
+
+        w_words = const.tile([P, CONVS, PASSES, 2 * OUT_CHANNELS], U8, align_bytes=64)
+        w_scales = const.tile([P, CONVS, PASSES, OUT_CHANNELS], U8, align_bytes=64)
+        nc.vector.memset(w_scales[:].bitcast(I32), 0)
+        x_tiles = {}
+
+        def load_image(b):
+            for c in range(PASSES):
+                x_tile = x_pool.tile([P, PACK * HEIGHT * WIDTH], BF16)
+                nc.sync.dma_start(out=x_tile[:], in_=x_rows[b, c])
+                x_tiles[(b, c)] = x_tile
+
+        def load_words(conv):
+            nc.sync.dma_start(
+                out=w_words[:, conv, :, :].bitcast(I32),
+                in_=words_in[conv].bitcast(I32).rearrange("c p n -> p c n"),
+            )
+
+        def load_scales(conv):
+            rows = scales_in[conv].bitcast(I32).rearrange("c q n -> q c n")
+            for quadrant in range(QUADRANTS):
+                nc.sync.dma_start(
+                    out=w_scales[32 * quadrant : 32 * quadrant + LIVE_ROWS, conv, :, :].bitcast(I32),
+                    in_=rows[LIVE_ROWS * quadrant : LIVE_ROWS * (quadrant + 1)],
+                )
+
+        load_image(0)
+        load_scales(0)
+        load_image(1)
+        load_words(0)
+        load_words(1)
+        load_scales(1)
+        load_image(2)
+        load_image(3)
+
+        identity = const.tile([P, P], BF16)
+        make_identity(nc, identity[:])
+        vector_cols_psum = setup_psum.tile([P, P], BF16)
+        nc.tensor.transpose(vector_cols_psum[:], vector_rows[:], identity[:])
+        vector_cols = const.tile([P, len(vectors), OUT_TILES], F32)
+        nc.vector.tensor_copy(
+            out=vector_cols[:].rearrange("p v j -> p (v j)"),
+            in_=vector_cols_psum[:, : len(vectors) * OUT_TILES],
+        )
+        scale = const.tile([P, CONVS, OUT_TILES], F32)
+        shift = const.tile([P, CONVS, OUT_TILES], F32)
+        var_eps = const.tile([P, OUT_TILES], F32)
+        std = const.tile([P, OUT_TILES], F32)
+        inv_std = const.tile([P, OUT_TILES], F32)
+        centred = const.tile([P, OUT_TILES], F32)
+        centred_scaled = const.tile([P, OUT_TILES], F32)
+        nc.vector.tensor_scalar_add(out=var_eps[:], in0=vector_cols[:, VAR, :], scalar1=EPS)
+        nc.scalar.sqrt(out=std[:], in_=var_eps[:])
+        nc.vector.tensor_sub(out=centred[:], in0=vector_cols[:, BK, :], in1=vector_cols[:, MEAN, :])
+        nc.vector.memset(scale[:, 1, :], 1.0)
+        nc.vector.tensor_copy(out=shift[:, 1, :], in_=vector_cols[:, BV, :])
+        nc.vector.reciprocal(out=inv_std[:], in_=std[:])
+        nc.vector.tensor_mul(out=scale[:, 0, :], in0=vector_cols[:, GAMMA, :], in1=inv_std[:])
+        nc.vector.tensor_mul(out=centred_scaled[:], in0=centred[:], in1=scale[:, 0, :])
+        nc.vector.tensor_add(out=shift[:, 0, :], in0=centred_scaled[:], in1=vector_cols[:, BETA, :])
+
+        for b in range(BATCH):
+            x_codes = quant.tile([P, PASSES, PIXELS], U32, align_bytes=64)
+            x_scales = quant.tile([P, PASSES, PIXELS], U8, align_bytes=64)
+            for c in range(PASSES):
+                row_pairs = x_tiles[(b, c)][:].rearrange("p (r two w) -> p r two w", two=2, w=WIDTH)
+                row_max = work.tile([P, PACK * PIXELS * 2], BF16)
+                nc.vector.tensor_max(
+                    out=row_max[:].rearrange("p (r w) -> p r w", w=WIDTH),
+                    in0=row_pairs[:, :, 0, :],
+                    in1=row_pairs[:, :, 1, :],
+                )
+                col_pairs = row_max[:].rearrange("p (t n two) -> p n t two", t=PACK, two=2)
+                grouped = work.tile([P, PIXELS * PACK], BF16, align_bytes=64)
+                nc.vector.tensor_max(
+                    out=grouped[:].rearrange("p (n t) -> p n t", t=PACK),
+                    in0=col_pairs[:, :, :, 0],
+                    in1=col_pairs[:, :, :, 1],
+                )
+                nc.vector.quantize_mx(
+                    out=x_codes[:, c, :].bitcast(FP8X4), scales=x_scales[:, c, :], in_=grouped[:]
+                )
+
+            for conv in range(CONVS):
+                out_rows = outs[conv][b].rearrange("(j p) h w -> p j (h w)", p=P)
+                for first in range(0, OUT_TILES, STORE_TILES):
+                    staged = stage.tile([P, STORE_TILES, PIXELS], F32)
+                    for s in range(STORE_TILES):
+                        j = first + s
+                        acc = psum.tile([P, PIXELS], F32)
+                        for c in range(PASSES):
+                            nc.tensor.matmul_mx(
+                                out=acc[:],
+                                lhsT=w_words[:, conv, c, 2 * P * j : 2 * P * (j + 1)].bitcast(FP4X4),
+                                lhsT_scale=w_scales[:, conv, c, P * j : P * (j + 1)],
+                                rhs=x_codes[:, c, :].bitcast(FP8X4),
+                                rhs_scale=x_scales[:, c, :],
+                                start=(c == 0),
+                                stop=(c == PASSES - 1),
+                            )
+                        nc.scalar.activation(
+                            out=staged[:, s, :],
+                            in_=acc[:],
+                            func=IDENTITY,
+                            bias=shift[:, conv, j : j + 1],
+                            scale=scale[:, conv, j : j + 1],
+                        )
+                    nc.sync.dma_start(out=out_rows[:, first : first + STORE_TILES, :], in_=staged[:])

@@ -24,6 +24,7 @@ CONVS = 2
 STORE_TILES = 4
 LIVE_ROWS = 4
 QUADRANTS = 4
+BIG_SLOTS = BATCH * PASSES + CONVS
 
 FLOPS = 2 * CONVS * BATCH * OUT_CHANNELS * CHANNELS * PIXELS
 
@@ -40,10 +41,9 @@ def tile_nonlocalnd_bn_pa_t_kernel(
     with ExitStack() as stack:
         stack.enter_context(tc.manual_schedule())
         const = stack.enter_context(tc.tile_pool(name="const", bufs=1))
-        x_pool = stack.enter_context(tc.tile_pool(name="x", bufs=BATCH * PASSES))
+        big = stack.enter_context(tc.tile_pool(name="big", bufs=BIG_SLOTS))
         work = stack.enter_context(tc.tile_pool(name="work", bufs=2))
         quant = stack.enter_context(tc.tile_pool(name="quant", bufs=BATCH))
-        stage = stack.enter_context(tc.tile_pool(name="stage", bufs=5))
         setup_psum = stack.enter_context(tc.psum_pool(name="setup_psum", bufs=1))
         psum = stack.enter_context(tc.psum_pool(name="psum", bufs=7))
 
@@ -64,7 +64,7 @@ def tile_nonlocalnd_bn_pa_t_kernel(
 
         def load_image(b):
             for c in range(PASSES):
-                x_tile = x_pool.tile([P, PACK * HEIGHT * WIDTH], BF16)
+                x_tile = big.tile([P, PACK * HEIGHT * WIDTH], BF16, tag="big")
                 nc.sync.dma_start(out=x_tile[:], in_=x_rows[b, c])
                 x_tiles[(b, c)] = x_tile
 
@@ -90,6 +90,35 @@ def tile_nonlocalnd_bn_pa_t_kernel(
         load_scales(1)
         load_image(2)
         load_image(3)
+
+        x_codes = {}
+        x_scales = {}
+
+        def pool_image(b):
+            codes = quant.tile([P, PASSES, PIXELS], U32, align_bytes=64)
+            planes = quant.tile([P, PASSES, PIXELS], U8, align_bytes=64)
+            x_codes[b] = codes
+            x_scales[b] = planes
+            for c in range(PASSES):
+                row_pairs = x_tiles[(b, c)][:].rearrange("p (r two w) -> p r two w", two=2, w=WIDTH)
+                row_max = work.tile([P, PACK * PIXELS * 2], BF16)
+                nc.vector.tensor_max(
+                    out=row_max[:].rearrange("p (r w) -> p r w", w=WIDTH),
+                    in0=row_pairs[:, :, 0, :],
+                    in1=row_pairs[:, :, 1, :],
+                )
+                col_pairs = row_max[:].rearrange("p (t n two) -> p n t two", t=PACK, two=2)
+                grouped = work.tile([P, PIXELS * PACK], BF16, align_bytes=64)
+                nc.vector.tensor_max(
+                    out=grouped[:].rearrange("p (n t) -> p n t", t=PACK),
+                    in0=col_pairs[:, :, :, 0],
+                    in1=col_pairs[:, :, :, 1],
+                )
+                nc.vector.quantize_mx(
+                    out=x_codes[b][:, c, :].bitcast(FP8X4), scales=x_scales[b][:, c, :], in_=grouped[:]
+                )
+
+        pool_image(0)
 
         identity = const.tile([P, P], BF16)
         make_identity(nc, identity[:])
@@ -118,49 +147,30 @@ def tile_nonlocalnd_bn_pa_t_kernel(
         nc.vector.tensor_add(out=shift[:, 0, :], in0=centred_scaled[:], in1=vector_cols[:, BETA, :])
 
         for b in range(BATCH):
-            x_codes = quant.tile([P, PASSES, PIXELS], U32, align_bytes=64)
-            x_scales = quant.tile([P, PASSES, PIXELS], U8, align_bytes=64)
-            for c in range(PASSES):
-                row_pairs = x_tiles[(b, c)][:].rearrange("p (r two w) -> p r two w", two=2, w=WIDTH)
-                row_max = work.tile([P, PACK * PIXELS * 2], BF16)
-                nc.vector.tensor_max(
-                    out=row_max[:].rearrange("p (r w) -> p r w", w=WIDTH),
-                    in0=row_pairs[:, :, 0, :],
-                    in1=row_pairs[:, :, 1, :],
-                )
-                col_pairs = row_max[:].rearrange("p (t n two) -> p n t two", t=PACK, two=2)
-                grouped = work.tile([P, PIXELS * PACK], BF16, align_bytes=64)
-                nc.vector.tensor_max(
-                    out=grouped[:].rearrange("p (n t) -> p n t", t=PACK),
-                    in0=col_pairs[:, :, :, 0],
-                    in1=col_pairs[:, :, :, 1],
-                )
-                nc.vector.quantize_mx(
-                    out=x_codes[:, c, :].bitcast(FP8X4), scales=x_scales[:, c, :], in_=grouped[:]
-                )
-
+            if b + 1 < BATCH:
+                pool_image(b + 1)
             for conv in range(CONVS):
                 out_rows = outs[conv][b].rearrange("(j p) h w -> p j (h w)", p=P)
-                for first in range(0, OUT_TILES, STORE_TILES):
-                    staged = stage.tile([P, STORE_TILES, PIXELS], F32)
-                    for s in range(STORE_TILES):
-                        j = first + s
-                        acc = psum.tile([P, PIXELS], F32)
-                        for c in range(PASSES):
-                            nc.tensor.matmul_mx(
-                                out=acc[:],
-                                lhsT=w_words[:, conv, c, 2 * P * j : 2 * P * (j + 1)].bitcast(FP4X4),
-                                lhsT_scale=w_scales[:, conv, c, P * j : P * (j + 1)],
-                                rhs=x_codes[:, c, :].bitcast(FP8X4),
-                                rhs_scale=x_scales[:, c, :],
-                                start=(c == 0),
-                                stop=(c == PASSES - 1),
-                            )
-                        nc.scalar.activation(
-                            out=staged[:, s, :],
-                            in_=acc[:],
-                            func=IDENTITY,
-                            bias=shift[:, conv, j : j + 1],
-                            scale=scale[:, conv, j : j + 1],
+                staged = big.tile([P, OUT_TILES, PIXELS], F32, tag="big")
+                for j in range(OUT_TILES):
+                    acc = psum.tile([P, PIXELS], F32)
+                    for c in range(PASSES):
+                        nc.tensor.matmul_mx(
+                            out=acc[:],
+                            lhsT=w_words[:, conv, c, 2 * P * j : 2 * P * (j + 1)].bitcast(FP4X4),
+                            lhsT_scale=w_scales[:, conv, c, P * j : P * (j + 1)],
+                            rhs=x_codes[b][:, c, :].bitcast(FP8X4),
+                            rhs_scale=x_scales[b][:, c, :],
+                            start=(c == 0),
+                            stop=(c == PASSES - 1),
                         )
-                    nc.sync.dma_start(out=out_rows[:, first : first + STORE_TILES, :], in_=staged[:])
+                    nc.scalar.activation(
+                        out=staged[:, j, :],
+                        in_=acc[:],
+                        func=IDENTITY,
+                        bias=shift[:, conv, j : j + 1],
+                        scale=scale[:, conv, j : j + 1],
+                    )
+                    if (j + 1) % STORE_TILES == 0:
+                        first = j + 1 - STORE_TILES
+                        nc.sync.dma_start(out=out_rows[:, first : j + 1, :], in_=staged[:, first : j + 1, :])

@@ -1,7 +1,6 @@
 from contextlib import ExitStack
 
 import concourse.mybir as mybir
-from concourse.masks import make_identity
 
 BF16 = mybir.dt.bfloat16
 F32 = mybir.dt.float32
@@ -21,7 +20,6 @@ PACK = 4
 PASSES = CHANNELS // (P * PACK)
 OUT_TILES = OUT_CHANNELS // P
 CONVS = 2
-STORE_TILES = 4
 LIVE_ROWS = 4
 QUADRANTS = 4
 BIG_SLOTS = BATCH * PASSES + CONVS
@@ -44,22 +42,19 @@ def tile_nonlocalnd_bn_pa_t_kernel(
         big = stack.enter_context(tc.tile_pool(name="big", bufs=BIG_SLOTS))
         work = stack.enter_context(tc.tile_pool(name="work", bufs=2))
         quant = stack.enter_context(tc.tile_pool(name="quant", bufs=BATCH))
-        setup_psum = stack.enter_context(tc.psum_pool(name="setup_psum", bufs=1))
-        psum = stack.enter_context(tc.psum_pool(name="psum", bufs=7))
+        psum = stack.enter_context(tc.psum_pool(name="psum", bufs=8))
 
         vectors = (bk, bv, k_gamma, k_beta, k_mean, k_var)
         BK, BV, GAMMA, BETA, MEAN, VAR = range(6)
-        vector_rows = const.tile([P, P], BF16)
-        nc.vector.memset(vector_rows[:], 0.0)
+        vector_raw = const.tile([P, len(vectors), 2 * OUT_TILES], BF16)
         for v, vector in enumerate(vectors):
             nc.scalar.dma_start(
-                out=vector_rows[OUT_TILES * v : OUT_TILES * (v + 1), :],
-                in_=vector.rearrange("(j p) -> j p", p=P),
+                out=vector_raw[:, v, :OUT_TILES], in_=vector.rearrange("(p j) -> p j", j=OUT_TILES)
             )
 
-        w_words = const.tile([P, CONVS, PASSES, 2 * OUT_CHANNELS], U8, align_bytes=64)
-        w_scales = const.tile([P, CONVS, PASSES, OUT_CHANNELS], U8, align_bytes=64)
-        nc.vector.memset(w_scales[:].bitcast(I32), 0)
+        raw_words = const.tile([P, CONVS, PASSES, 2 * OUT_CHANNELS], U8, align_bytes=64)
+        raw_scales = const.tile([P, CONVS, PASSES, OUT_CHANNELS], U8, align_bytes=64)
+        nc.vector.memset(raw_scales[:].bitcast(I32), 0)
         x_tiles = {}
 
         def load_image(b):
@@ -70,7 +65,7 @@ def tile_nonlocalnd_bn_pa_t_kernel(
 
         def load_words(conv):
             nc.sync.dma_start(
-                out=w_words[:, conv, :, :].bitcast(I32),
+                out=raw_words[:, conv, :, :].bitcast(I32),
                 in_=words_in[conv].bitcast(I32).rearrange("c p n -> p c n"),
             )
 
@@ -78,18 +73,34 @@ def tile_nonlocalnd_bn_pa_t_kernel(
             rows = scales_in[conv].bitcast(I32).rearrange("c q n -> q c n")
             for quadrant in range(QUADRANTS):
                 nc.sync.dma_start(
-                    out=w_scales[32 * quadrant : 32 * quadrant + LIVE_ROWS, conv, :, :].bitcast(I32),
+                    out=raw_scales[32 * quadrant : 32 * quadrant + LIVE_ROWS, conv, :, :].bitcast(I32),
                     in_=rows[LIVE_ROWS * quadrant : LIVE_ROWS * (quadrant + 1)],
                 )
 
+        load_words(0)
+        load_words(1)
         load_image(0)
         load_scales(0)
         load_image(1)
-        load_words(0)
-        load_words(1)
         load_scales(1)
         load_image(2)
         load_image(3)
+
+        w_words = const.tile([P, CONVS, PASSES, 2 * OUT_CHANNELS], U8, align_bytes=64)
+        w_scales = const.tile([P, CONVS, PASSES, OUT_CHANNELS], U8, align_bytes=64)
+
+        def reorder_words(conv):
+            for c in range(PASSES):
+                nc.vector.tensor_copy(
+                    out=w_words[:, conv, c, :].rearrange("p (j m two) -> p j m two", j=OUT_TILES, two=2),
+                    in_=raw_words[:, conv, c, :].rearrange("p (m j two) -> p j m two", j=OUT_TILES, two=2),
+                )
+
+        def reorder_scales(conv):
+            nc.vector.tensor_copy(
+                out=w_scales[:, conv, :, :].rearrange("p c (j m) -> p c j m", j=OUT_TILES),
+                in_=raw_scales[:, conv, :, :].rearrange("p c (m j) -> p c j m", j=OUT_TILES),
+            )
 
         x_codes = {}
         x_scales = {}
@@ -118,17 +129,14 @@ def tile_nonlocalnd_bn_pa_t_kernel(
                     out=x_codes[b][:, c, :].bitcast(FP8X4), scales=x_scales[b][:, c, :], in_=grouped[:]
                 )
 
+        reorder_words(0)
+        reorder_words(1)
         pool_image(0)
+        reorder_scales(0)
+        reorder_scales(1)
 
-        identity = const.tile([P, P], BF16)
-        make_identity(nc, identity[:])
-        vector_cols_psum = setup_psum.tile([P, P], BF16)
-        nc.tensor.transpose(vector_cols_psum[:], vector_rows[:], identity[:])
         vector_cols = const.tile([P, len(vectors), OUT_TILES], F32)
-        nc.vector.tensor_copy(
-            out=vector_cols[:].rearrange("p v j -> p (v j)"),
-            in_=vector_cols_psum[:, : len(vectors) * OUT_TILES],
-        )
+        nc.vector.tensor_copy(out=vector_cols[:], in_=vector_raw[:, :, :OUT_TILES])
         scale = const.tile([P, CONVS, OUT_TILES], F32)
         shift = const.tile([P, CONVS, OUT_TILES], F32)
         var_eps = const.tile([P, OUT_TILES], F32)
@@ -150,7 +158,6 @@ def tile_nonlocalnd_bn_pa_t_kernel(
             if b + 1 < BATCH:
                 pool_image(b + 1)
             for conv in range(CONVS):
-                out_rows = outs[conv][b].rearrange("(j p) h w -> p j (h w)", p=P)
                 staged = big.tile([P, OUT_TILES, PIXELS], F32, tag="big")
                 for j in range(OUT_TILES):
                     acc = psum.tile([P, PIXELS], F32)
@@ -171,6 +178,7 @@ def tile_nonlocalnd_bn_pa_t_kernel(
                         bias=shift[:, conv, j : j + 1],
                         scale=scale[:, conv, j : j + 1],
                     )
-                    if (j + 1) % STORE_TILES == 0:
-                        first = j + 1 - STORE_TILES
-                        nc.sync.dma_start(out=out_rows[:, first : j + 1, :], in_=staged[:, first : j + 1, :])
+                nc.sync.dma_start(
+                    out=outs[conv][b].rearrange("(p j) h w -> p (j h w)", j=OUT_TILES),
+                    in_=staged[:].rearrange("p j n -> p (j n)"),
+                )

@@ -10,6 +10,9 @@ U8 = mybir.dt.uint8
 FP8X4 = mybir.dt.float8_e4m3fn_x4
 FP4X4 = mybir.dt.float4_e2m1fn_x4
 IDENTITY = mybir.ActivationFunctionType.Identity
+SQRT = mybir.ActivationFunctionType.Sqrt
+MULT = mybir.AluOpType.mult
+ADD = mybir.AluOpType.add
 
 BATCH, CHANNELS, HEIGHT, WIDTH, OUT_CHANNELS = 4, 1024, 64, 32, 1024
 EPS = 1e-5
@@ -20,6 +23,9 @@ PACK = 4
 PASSES = CHANNELS // (P * PACK)
 OUT_TILES = OUT_CHANNELS // P
 CONVS = 2
+RUN = 4
+HALVES = OUT_TILES // RUN
+UNITS = BATCH * PASSES
 LIVE_ROWS = 4
 QUADRANTS = 4
 BIG_SLOTS = BATCH * PASSES + CONVS
@@ -49,19 +55,21 @@ def tile_nonlocalnd_bn_pa_t_kernel(
         vector_raw = const.tile([P, len(vectors), 2 * OUT_TILES], BF16)
         for v, vector in enumerate(vectors):
             nc.scalar.dma_start(
-                out=vector_raw[:, v, :OUT_TILES], in_=vector.rearrange("(p j) -> p j", j=OUT_TILES)
+                out=vector_raw[:, v, :OUT_TILES].rearrange("p (h j) -> p h j", j=RUN),
+                in_=vector.rearrange("(h p j) -> p h j", p=P, j=RUN),
             )
+        std = const.tile([P, OUT_TILES], F32)
+        nc.scalar.activation(out=std[:], in_=vector_raw[:, VAR, :OUT_TILES], func=SQRT, bias=EPS)
 
         raw_words = const.tile([P, CONVS, PASSES, 2 * OUT_CHANNELS], U8, align_bytes=64)
         raw_scales = const.tile([P, CONVS, PASSES, OUT_CHANNELS], U8, align_bytes=64)
         nc.vector.memset(raw_scales[:].bitcast(I32), 0)
-        x_tiles = {}
+        x_tiles = []
 
-        def load_image(b):
-            for c in range(PASSES):
-                x_tile = big.tile([P, PACK * HEIGHT * WIDTH], BF16, tag="big")
-                nc.sync.dma_start(out=x_tile[:], in_=x_rows[b, c])
-                x_tiles[(b, c)] = x_tile
+        def load_x(u):
+            x_tile = big.tile([P, PACK * HEIGHT * WIDTH], BF16, tag="big")
+            nc.sync.dma_start(out=x_tile[:], in_=x_rows[u // PASSES, u % PASSES])
+            x_tiles.append(x_tile)
 
         def load_words(conv):
             nc.sync.dma_start(
@@ -79,85 +87,97 @@ def tile_nonlocalnd_bn_pa_t_kernel(
 
         load_words(0)
         load_words(1)
-        load_image(0)
+        load_x(0)
+        load_x(1)
         load_scales(0)
-        load_image(1)
+        load_x(2)
         load_scales(1)
-        load_image(2)
-        load_image(3)
+        for u in range(3, UNITS):
+            load_x(u)
 
         w_words = const.tile([P, CONVS, PASSES, 2 * OUT_CHANNELS], U8, align_bytes=64)
         w_scales = const.tile([P, CONVS, PASSES, OUT_CHANNELS], U8, align_bytes=64)
 
         def reorder_words(conv):
             for c in range(PASSES):
-                nc.vector.tensor_copy(
-                    out=w_words[:, conv, c, :].rearrange("p (j m two) -> p j m two", j=OUT_TILES, two=2),
-                    in_=raw_words[:, conv, c, :].rearrange("p (m j two) -> p j m two", j=OUT_TILES, two=2),
-                )
+                for h in range(HALVES):
+                    half = slice(2 * RUN * P * h, 2 * RUN * P * (h + 1))
+                    nc.vector.tensor_copy(
+                        out=w_words[:, conv, c, half].rearrange("p (j m two) -> p j m two", j=RUN, two=2),
+                        in_=raw_words[:, conv, c, half].rearrange("p (m j two) -> p j m two", j=RUN, two=2),
+                    )
 
         def reorder_scales(conv):
             nc.vector.tensor_copy(
-                out=w_scales[:, conv, :, :].rearrange("p c (j m) -> p c j m", j=OUT_TILES),
-                in_=raw_scales[:, conv, :, :].rearrange("p c (m j) -> p c j m", j=OUT_TILES),
+                out=w_scales[:, conv, :, :].rearrange("p c (h j m) -> p (c h) j m", h=HALVES, j=RUN),
+                in_=raw_scales[:, conv, :, :].rearrange("p c (h m j) -> p (c h) j m", h=HALVES, j=RUN),
             )
 
-        x_codes = {}
-        x_scales = {}
+        x_codes = []
+        x_scales = []
+        row_maxes = {}
+        groupeds = {}
 
-        def pool_image(b):
-            codes = quant.tile([P, PASSES, PIXELS], U32, align_bytes=64)
-            planes = quant.tile([P, PASSES, PIXELS], U8, align_bytes=64)
-            x_codes[b] = codes
-            x_scales[b] = planes
-            for c in range(PASSES):
-                row_pairs = x_tiles[(b, c)][:].rearrange("p (r two w) -> p r two w", two=2, w=WIDTH)
-                row_max = work.tile([P, PACK * PIXELS * 2], BF16)
-                nc.vector.tensor_max(
-                    out=row_max[:].rearrange("p (r w) -> p r w", w=WIDTH),
-                    in0=row_pairs[:, :, 0, :],
-                    in1=row_pairs[:, :, 1, :],
-                )
-                col_pairs = row_max[:].rearrange("p (t n two) -> p n t two", t=PACK, two=2)
-                grouped = work.tile([P, PIXELS * PACK], BF16, align_bytes=64)
-                nc.vector.tensor_max(
-                    out=grouped[:].rearrange("p (n t) -> p n t", t=PACK),
-                    in0=col_pairs[:, :, :, 0],
-                    in1=col_pairs[:, :, :, 1],
-                )
-                nc.vector.quantize_mx(
-                    out=x_codes[b][:, c, :].bitcast(FP8X4), scales=x_scales[b][:, c, :], in_=grouped[:]
-                )
+        def max_rows(u):
+            row_pairs = x_tiles[u][:].rearrange("p (r two w) -> p r two w", two=2, w=WIDTH)
+            row_max = work.tile([P, PACK * PIXELS * 2], BF16)
+            nc.vector.tensor_max(
+                out=row_max[:].rearrange("p (r w) -> p r w", w=WIDTH),
+                in0=row_pairs[:, :, 0, :],
+                in1=row_pairs[:, :, 1, :],
+            )
+            row_maxes[u] = row_max
 
-        reorder_words(0)
-        reorder_words(1)
-        pool_image(0)
-        reorder_scales(0)
-        reorder_scales(1)
+        def max_columns(u):
+            col_pairs = row_maxes[u][:].rearrange("p (t n two) -> p n t two", t=PACK, two=2)
+            grouped = work.tile([P, PIXELS * PACK], BF16, align_bytes=64)
+            nc.vector.tensor_max(
+                out=grouped[:].rearrange("p (n t) -> p n t", t=PACK),
+                in0=col_pairs[:, :, :, 0],
+                in1=col_pairs[:, :, :, 1],
+            )
+            groupeds[u] = grouped
 
-        vector_cols = const.tile([P, len(vectors), OUT_TILES], F32)
-        nc.vector.tensor_copy(out=vector_cols[:], in_=vector_raw[:, :, :OUT_TILES])
+        def quantise(u):
+            b, c = divmod(u, PASSES)
+            if c == 0:
+                codes = quant.tile([P, PASSES, PIXELS], U32, align_bytes=64)
+                planes = quant.tile([P, PASSES, PIXELS], U8, align_bytes=64)
+                x_codes.append(codes)
+                x_scales.append(planes)
+            nc.vector.quantize_mx(
+                out=x_codes[b][:, c, :].bitcast(FP8X4), scales=x_scales[b][:, c, :], in_=groupeds[u][:]
+            )
+
         scale = const.tile([P, CONVS, OUT_TILES], F32)
         shift = const.tile([P, CONVS, OUT_TILES], F32)
-        var_eps = const.tile([P, OUT_TILES], F32)
-        std = const.tile([P, OUT_TILES], F32)
         inv_std = const.tile([P, OUT_TILES], F32)
         centred = const.tile([P, OUT_TILES], F32)
         centred_scaled = const.tile([P, OUT_TILES], F32)
-        nc.vector.tensor_scalar_add(out=var_eps[:], in0=vector_cols[:, VAR, :], scalar1=EPS)
-        nc.scalar.sqrt(out=std[:], in_=var_eps[:])
-        nc.vector.tensor_sub(out=centred[:], in0=vector_cols[:, BK, :], in1=vector_cols[:, MEAN, :])
-        nc.vector.memset(scale[:, 1, :], 1.0)
-        nc.vector.tensor_copy(out=shift[:, 1, :], in_=vector_cols[:, BV, :])
-        nc.vector.reciprocal(out=inv_std[:], in_=std[:])
-        nc.vector.tensor_mul(out=scale[:, 0, :], in0=vector_cols[:, GAMMA, :], in1=inv_std[:])
-        nc.vector.tensor_mul(out=centred_scaled[:], in0=centred[:], in1=scale[:, 0, :])
-        nc.vector.tensor_add(out=shift[:, 0, :], in0=centred_scaled[:], in1=vector_cols[:, BETA, :])
 
-        for b in range(BATCH):
-            if b + 1 < BATCH:
-                pool_image(b + 1)
+        def column(v):
+            return vector_raw[:, v, :OUT_TILES]
+
+        small_work = [
+            lambda: nc.vector.reciprocal(out=inv_std[:], in_=std[:]),
+            lambda: nc.vector.tensor_sub(out=centred[:], in0=column(BK), in1=column(MEAN)),
+            lambda: nc.vector.tensor_mul(out=scale[:, 0, :], in0=column(GAMMA), in1=inv_std[:]),
+            lambda: nc.vector.memset(scale[:, 1, :], 1.0),
+            lambda: nc.vector.tensor_mul(out=centred_scaled[:], in0=centred[:], in1=scale[:, 0, :]),
+            lambda: nc.vector.tensor_copy(out=shift[:, 1, :], in_=column(BV)),
+            lambda: nc.vector.tensor_add(out=shift[:, 0, :], in0=centred_scaled[:], in1=column(BETA)),
+        ]
+
+        small_done = []
+
+        def next_small():
+            if len(small_done) < len(small_work):
+                small_work[len(small_done)]()
+                small_done.append(True)
+
+        def convolve(b, vector_helps):
             for conv in range(CONVS):
+                out_halves = outs[conv][b].rearrange("(h p j) r w -> h p (j r w)", p=P, j=RUN)
                 staged = big.tile([P, OUT_TILES, PIXELS], F32, tag="big")
                 for j in range(OUT_TILES):
                     acc = psum.tile([P, PIXELS], F32)
@@ -171,14 +191,46 @@ def tile_nonlocalnd_bn_pa_t_kernel(
                             start=(c == 0),
                             stop=(c == PASSES - 1),
                         )
-                    nc.scalar.activation(
-                        out=staged[:, j, :],
-                        in_=acc[:],
-                        func=IDENTITY,
-                        bias=shift[:, conv, j : j + 1],
-                        scale=scale[:, conv, j : j + 1],
-                    )
-                nc.sync.dma_start(
-                    out=outs[conv][b].rearrange("(p j) h w -> p (j h w)", j=OUT_TILES),
-                    in_=staged[:].rearrange("p j n -> p (j n)"),
-                )
+                    if vector_helps and j % 2 == 1:
+                        nc.vector.tensor_scalar(
+                            out=staged[:, j, :],
+                            in0=acc[:],
+                            scalar1=scale[:, conv, j : j + 1],
+                            scalar2=shift[:, conv, j : j + 1],
+                            op0=MULT,
+                            op1=ADD,
+                        )
+                    else:
+                        nc.scalar.activation(
+                            out=staged[:, j, :],
+                            in_=acc[:],
+                            func=IDENTITY,
+                            bias=shift[:, conv, j : j + 1],
+                            scale=scale[:, conv, j : j + 1],
+                        )
+                    if j % RUN == RUN - 1:
+                        h = j // RUN
+                        nc.sync.dma_start(
+                            out=out_halves[h],
+                            in_=staged[:, RUN * h : RUN * (h + 1), :].rearrange("p j n -> p (j n)"),
+                        )
+
+        reorder_words(0)
+        reorder_words(1)
+        for s in range(UNITS + 2):
+            if 0 <= s - 2:
+                quantise(s - 2)
+                next_small()
+            if 0 <= s - 1 < UNITS:
+                max_columns(s - 1)
+                next_small()
+            if s < UNITS:
+                max_rows(s)
+                next_small()
+            if s == 2:
+                reorder_scales(0)
+            if s == 3:
+                reorder_scales(1)
+            if s >= 3 and s % 2 == 1:
+                b = (s - 3) // 2
+                convolve(b, vector_helps=(b == BATCH - 1))

@@ -72,10 +72,8 @@ def tile_nonlocalnd_bn_pa_t_kernel(
             x_tiles.append(x_tile)
 
         def load_words(conv):
-            nc.sync.dma_start(
-                out=raw_words[:, conv, :, :].bitcast(I32),
-                in_=words_in[conv].bitcast(I32).rearrange("c p n -> p c n"),
-            )
+            for c in range(PASSES):
+                nc.sync.dma_start(out=raw_words[:, conv, c, :].bitcast(I32), in_=words_in[conv][c].bitcast(I32))
 
         def load_scales(conv):
             rows = scales_in[conv].bitcast(I32).rearrange("c q n -> q c n")
@@ -175,22 +173,37 @@ def tile_nonlocalnd_bn_pa_t_kernel(
                 small_work[len(small_done)]()
                 small_done.append(True)
 
+        def multiply(acc, b, conv, j, c):
+            nc.tensor.matmul_mx(
+                out=acc[:],
+                lhsT=w_words[:, conv, c, 2 * P * j : 2 * P * (j + 1)].bitcast(FP4X4),
+                lhsT_scale=w_scales[:, conv, c, P * j : P * (j + 1)],
+                rhs=x_codes[b][:, c, :].bitcast(FP8X4),
+                rhs_scale=x_scales[b][:, c, :],
+                start=(c == 0),
+                stop=(c == PASSES - 1),
+            )
+
+        opened = []
+
+        def open_k(b):
+            for j in range(OUT_TILES):
+                acc = psum.tile([P, PIXELS], F32)
+                multiply(acc, b, 0, j, 0)
+                opened.append(acc)
+
         def convolve(b, vector_helps):
             for conv in range(CONVS):
-                out_halves = outs[conv][b].rearrange("(h p j) r w -> h p (j r w)", p=P, j=RUN)
+                out_rows = outs[conv][b].rearrange("(h p j) r w -> h p j (r w)", p=P, j=RUN)
                 staged = big.tile([P, OUT_TILES, PIXELS], F32, tag="big")
+                first = 0
                 for j in range(OUT_TILES):
-                    acc = psum.tile([P, PIXELS], F32)
-                    for c in range(PASSES):
-                        nc.tensor.matmul_mx(
-                            out=acc[:],
-                            lhsT=w_words[:, conv, c, 2 * P * j : 2 * P * (j + 1)].bitcast(FP4X4),
-                            lhsT_scale=w_scales[:, conv, c, P * j : P * (j + 1)],
-                            rhs=x_codes[b][:, c, :].bitcast(FP8X4),
-                            rhs_scale=x_scales[b][:, c, :],
-                            start=(c == 0),
-                            stop=(c == PASSES - 1),
-                        )
+                    if conv == 0:
+                        acc = opened[OUT_TILES * b + j]
+                    else:
+                        acc = psum.tile([P, PIXELS], F32)
+                        multiply(acc, b, conv, j, 0)
+                    multiply(acc, b, conv, j, 1)
                     if vector_helps and j % 2 == 1:
                         nc.vector.tensor_scalar(
                             out=staged[:, j, :],
@@ -208,12 +221,14 @@ def tile_nonlocalnd_bn_pa_t_kernel(
                             bias=shift[:, conv, j : j + 1],
                             scale=scale[:, conv, j : j + 1],
                         )
-                    if j % RUN == RUN - 1:
+                    at_end = vector_helps and conv == CONVS - 1 and j >= OUT_TILES - RUN
+                    if (j + 1) % (RUN // 2 if at_end else RUN) == 0:
                         h = j // RUN
                         nc.sync.dma_start(
-                            out=out_halves[h],
-                            in_=staged[:, RUN * h : RUN * (h + 1), :].rearrange("p j n -> p (j n)"),
+                            out=out_rows[h][:, first - RUN * h : j + 1 - RUN * h, :].rearrange("p j n -> p (j n)"),
+                            in_=staged[:, first : j + 1, :].rearrange("p j n -> p (j n)"),
                         )
+                        first = j + 1
 
         reorder_words(0)
         reorder_words(1)
@@ -231,6 +246,8 @@ def tile_nonlocalnd_bn_pa_t_kernel(
                 reorder_scales(0)
             if s == 3:
                 reorder_scales(1)
+            if s >= 2 and s % 2 == 0:
+                open_k((s - 2) // 2)
             if s >= 3 and s % 2 == 1:
                 b = (s - 3) // 2
                 convolve(b, vector_helps=(b == BATCH - 1))

@@ -23,7 +23,7 @@ PACK = 4
 PASSES = CHANNELS // (P * PACK)
 OUT_TILES = OUT_CHANNELS // P
 CONVS = 2
-RUN = 4
+RUN = 8
 HALVES = OUT_TILES // RUN
 UNITS = BATCH * PASSES
 LIVE_ROWS = 4

@@ -23,12 +23,23 @@ PACK = 4
 PASSES = CHANNELS // (P * PACK)
 OUT_TILES = OUT_CHANNELS // P
 CONVS = 2
-RUN = 8
-HALVES = OUT_TILES // RUN
 UNITS = BATCH * PASSES
+UNIT_COLUMNS = PACK * HEIGHT * WIDTH
 LIVE_ROWS = 4
 QUADRANTS = 4
-BIG_SLOTS = BATCH * PASSES + CONVS
+SLOT = UNIT_COLUMNS * 2
+
+LOADS = ((0,), (1,), (2,), (3,), (4, 5), (6, 7))
+STORES = (
+    (1, (0,), 8 * SLOT),
+    (0, (0, 1), 0),
+    (1, (1,), 9 * SLOT),
+    (0, (2,), 2 * SLOT),
+    (1, (2,), 3 * SLOT),
+    (0, (3,), 4 * SLOT),
+    (1, (3,), 5 * SLOT),
+)
+CONV_ORDER = ((0, 1), (0, 1), (0, 1), (0, 1))
 
 FLOPS = 2 * CONVS * BATCH * OUT_CHANNELS * CHANNELS * PIXELS
 
@@ -40,40 +51,50 @@ def tile_nonlocalnd_bn_pa_t_kernel(
     words_in = (wk_words, wv_words)
     scales_in = (wk_scales, wv_scales)
     outs = (out_0, out_1)
-    x_rows = x.rearrange("b (c p t) h w -> b c p (t h w)", p=P, t=PACK)
 
     with ExitStack() as stack:
         stack.enter_context(tc.manual_schedule())
         const = stack.enter_context(tc.tile_pool(name="const", bufs=1))
-        big = stack.enter_context(tc.tile_pool(name="big", bufs=BIG_SLOTS))
+        region = stack.enter_context(tc.tile_pool(name="region", bufs=1))
         work = stack.enter_context(tc.tile_pool(name="work", bufs=2))
         quant = stack.enter_context(tc.tile_pool(name="quant", bufs=BATCH))
         psum = stack.enter_context(tc.psum_pool(name="psum", bufs=8))
 
-        vectors = (bk, bv, k_gamma, k_beta, k_mean, k_var)
-        BK, BV, GAMMA, BETA, MEAN, VAR = range(6)
+        vectors = (k_var, k_gamma, bk, k_mean, k_beta, bv)
+        VAR, GAMMA, BK, MEAN, BETA, BV = range(6)
         vector_raw = const.tile([P, len(vectors), 2 * OUT_TILES], BF16)
-        for v, vector in enumerate(vectors):
-            nc.scalar.dma_start(
-                out=vector_raw[:, v, :OUT_TILES].rearrange("p (h j) -> p h j", j=RUN),
-                in_=vector.rearrange("(h p j) -> p h j", p=P, j=RUN),
-            )
         std = const.tile([P, OUT_TILES], F32)
-        nc.scalar.activation(out=std[:], in_=vector_raw[:, VAR, :OUT_TILES], func=SQRT, bias=EPS)
+
+        def load_vectors():
+            for v, vector in enumerate(vectors):
+                nc.scalar.dma_start(
+                    out=vector_raw[:, v, :OUT_TILES],
+                    in_=vector.rearrange("(p j) -> p j", p=P),
+                )
+            nc.scalar.activation(out=std[:], in_=vector_raw[:, VAR, :OUT_TILES], func=SQRT, bias=EPS)
 
         raw_words = const.tile([P, CONVS, PASSES, 2 * OUT_CHANNELS], U8, align_bytes=64)
         raw_scales = const.tile([P, CONVS, PASSES, OUT_CHANNELS], U8, align_bytes=64)
         nc.vector.memset(raw_scales[:].bitcast(I32), 0)
-        x_tiles = []
+        x_units = []
 
-        def load_x(u):
-            x_tile = big.tile([P, PACK * HEIGHT * WIDTH], BF16, tag="big")
-            nc.sync.dma_start(out=x_tile[:], in_=x_rows[u // PASSES, u % PASSES])
-            x_tiles.append(x_tile)
+        def load_units(units):
+            b, c = divmod(units[0], PASSES)
+            x_tile = region.tile(
+                [P, len(units), UNIT_COLUMNS], BF16, name="x_tile%d" % units[0], offset=units[0] * SLOT
+            )
+            nc.sync.dma_start(
+                out=x_tile[:],
+                in_=x[b].rearrange("(c p t) h w -> p c (t h w)", p=P, t=PACK)[:, c : c + len(units), :],
+            )
+            for i in range(len(units)):
+                x_units.append(x_tile[:, i, :])
 
         def load_words(conv):
-            for c in range(PASSES):
-                nc.sync.dma_start(out=raw_words[:, conv, c, :].bitcast(I32), in_=words_in[conv][c].bitcast(I32))
+            nc.sync.dma_start(
+                out=raw_words[:, conv, :, :].bitcast(I32),
+                in_=words_in[conv].bitcast(I32).rearrange("c p n -> p c n"),
+            )
 
         def load_scales(conv):
             rows = scales_in[conv].bitcast(I32).rearrange("c q n -> q c n")
@@ -85,30 +106,30 @@ def tile_nonlocalnd_bn_pa_t_kernel(
 
         load_words(0)
         load_words(1)
-        load_x(0)
-        load_x(1)
+        load_units(LOADS[0])
         load_scales(0)
-        load_x(2)
+        load_units(LOADS[1])
+        load_vectors()
+        load_units(LOADS[2])
+        load_units(LOADS[3])
         load_scales(1)
-        for u in range(3, UNITS):
-            load_x(u)
+        for units in LOADS[4:]:
+            load_units(units)
 
         w_words = const.tile([P, CONVS, PASSES, 2 * OUT_CHANNELS], U8, align_bytes=64)
         w_scales = const.tile([P, CONVS, PASSES, OUT_CHANNELS], U8, align_bytes=64)
 
         def reorder_words(conv):
             for c in range(PASSES):
-                for h in range(HALVES):
-                    half = slice(2 * RUN * P * h, 2 * RUN * P * (h + 1))
-                    nc.vector.tensor_copy(
-                        out=w_words[:, conv, c, half].rearrange("p (j m two) -> p j m two", j=RUN, two=2),
-                        in_=raw_words[:, conv, c, half].rearrange("p (m j two) -> p j m two", j=RUN, two=2),
-                    )
+                nc.vector.tensor_copy(
+                    out=w_words[:, conv, c, :].rearrange("p (j m two) -> p j m two", j=OUT_TILES, two=2),
+                    in_=raw_words[:, conv, c, :].rearrange("p (m j two) -> p j m two", j=OUT_TILES, two=2),
+                )
 
         def reorder_scales(conv):
             nc.vector.tensor_copy(
-                out=w_scales[:, conv, :, :].rearrange("p c (h j m) -> p (c h) j m", h=HALVES, j=RUN),
-                in_=raw_scales[:, conv, :, :].rearrange("p c (h m j) -> p (c h) j m", h=HALVES, j=RUN),
+                out=w_scales[:, conv, :, :].rearrange("p c (j m) -> p c j m", j=OUT_TILES),
+                in_=raw_scales[:, conv, :, :].rearrange("p c (m j) -> p c j m", j=OUT_TILES),
             )
 
         x_codes = []
@@ -117,7 +138,7 @@ def tile_nonlocalnd_bn_pa_t_kernel(
         groupeds = {}
 
         def max_rows(u):
-            row_pairs = x_tiles[u][:].rearrange("p (r two w) -> p r two w", two=2, w=WIDTH)
+            row_pairs = x_units[u].rearrange("p (r two w) -> p r two w", two=2, w=WIDTH)
             row_max = work.tile([P, PACK * PIXELS * 2], BF16)
             nc.vector.tensor_max(
                 out=row_max[:].rearrange("p (r w) -> p r w", w=WIDTH),
@@ -165,13 +186,13 @@ def tile_nonlocalnd_bn_pa_t_kernel(
             lambda: nc.vector.tensor_copy(out=shift[:, 1, :], in_=column(BV)),
             lambda: nc.vector.tensor_add(out=shift[:, 0, :], in0=centred_scaled[:], in1=column(BETA)),
         ]
-
         small_done = []
 
         def next_small():
-            if len(small_done) < len(small_work):
-                small_work[len(small_done)]()
-                small_done.append(True)
+            for repeat in range(2):
+                if len(small_done) < len(small_work):
+                    small_work[len(small_done)]()
+                    small_done.append(True)
 
         def multiply(acc, b, conv, j, c):
             nc.tensor.matmul_mx(
@@ -186,19 +207,30 @@ def tile_nonlocalnd_bn_pa_t_kernel(
 
         opened = []
 
-        def open_k(b):
+        def open_first(b):
             for j in range(OUT_TILES):
                 acc = psum.tile([P, PIXELS], F32)
-                multiply(acc, b, 0, j, 0)
+                multiply(acc, b, CONV_ORDER[b][0], j, 0)
                 opened.append(acc)
 
+        staged_tiles = {}
+
+        def staged_for(conv, b):
+            for i, (store_conv, images, offset) in enumerate(STORES):
+                if store_conv == conv and b in images:
+                    if i not in staged_tiles:
+                        staged = region.tile(
+                            [P, len(images), OUT_TILES, PIXELS], F32, name="staged%d" % i, offset=offset
+                        )
+                        staged_tiles[i] = staged
+                    return staged_tiles[i], images, images.index(b)
+            raise ValueError("no store")
+
         def convolve(b, vector_helps):
-            for conv in range(CONVS):
-                out_rows = outs[conv][b].rearrange("(h p j) r w -> h p j (r w)", p=P, j=RUN)
-                staged = big.tile([P, OUT_TILES, PIXELS], F32, tag="big")
-                first = 0
+            for turn, conv in enumerate(CONV_ORDER[b]):
+                staged, images, place = staged_for(conv, b)
                 for j in range(OUT_TILES):
-                    if conv == 0:
+                    if turn == 0:
                         acc = opened[OUT_TILES * b + j]
                     else:
                         acc = psum.tile([P, PIXELS], F32)
@@ -206,7 +238,7 @@ def tile_nonlocalnd_bn_pa_t_kernel(
                     multiply(acc, b, conv, j, 1)
                     if vector_helps and j % 2 == 1:
                         nc.vector.tensor_scalar(
-                            out=staged[:, j, :],
+                            out=staged[:, place, j, :],
                             in0=acc[:],
                             scalar1=scale[:, conv, j : j + 1],
                             scalar2=shift[:, conv, j : j + 1],
@@ -215,20 +247,19 @@ def tile_nonlocalnd_bn_pa_t_kernel(
                         )
                     else:
                         nc.scalar.activation(
-                            out=staged[:, j, :],
+                            out=staged[:, place, j, :],
                             in_=acc[:],
                             func=IDENTITY,
                             bias=shift[:, conv, j : j + 1],
                             scale=scale[:, conv, j : j + 1],
                         )
-                    at_end = vector_helps and conv == CONVS - 1 and j >= OUT_TILES - RUN
-                    if (j + 1) % (RUN // 2 if at_end else RUN) == 0:
-                        h = j // RUN
-                        nc.sync.dma_start(
-                            out=out_rows[h][:, first - RUN * h : j + 1 - RUN * h, :].rearrange("p j n -> p (j n)"),
-                            in_=staged[:, first : j + 1, :].rearrange("p j n -> p (j n)"),
-                        )
-                        first = j + 1
+                if b == images[-1]:
+                    nc.sync.dma_start(
+                        out=outs[conv][images[0] : images[-1] + 1].rearrange(
+                            "b (p j) r w -> p b (j r w)", p=P
+                        ),
+                        in_=staged[:].rearrange("p b j n -> p b (j n)"),
+                    )
 
         reorder_words(0)
         reorder_words(1)
@@ -236,18 +267,20 @@ def tile_nonlocalnd_bn_pa_t_kernel(
             if 0 <= s - 2:
                 quantise(s - 2)
                 next_small()
-            if 0 <= s - 1 < UNITS:
-                max_columns(s - 1)
-                next_small()
-            if s < UNITS:
-                max_rows(s)
-                next_small()
-            if s == 2:
-                reorder_scales(0)
             if s == 3:
                 reorder_scales(1)
+            if 0 <= s - 1 < UNITS:
+                max_columns(s - 1)
+                if s >= 2:
+                    next_small()
+            if s < UNITS:
+                max_rows(s)
+                if s >= 1:
+                    next_small()
+            if s == 0:
+                reorder_scales(0)
             if s >= 2 and s % 2 == 0:
-                open_k((s - 2) // 2)
+                open_first((s - 2) // 2)
             if s >= 3 and s % 2 == 1:
                 b = (s - 3) // 2
                 convolve(b, vector_helps=(b == BATCH - 1))

@@ -1,6 +1,7 @@
 from contextlib import ExitStack
 
 import concourse.mybir as mybir
+from concourse.masks import make_identity
 
 BF16 = mybir.dt.bfloat16
 F32 = mybir.dt.float32
@@ -27,6 +28,7 @@ UNITS = BATCH * PASSES
 UNIT_COLUMNS = PACK * HEIGHT * WIDTH
 LIVE_ROWS = 4
 QUADRANTS = 4
+ROW_STEP = 4
 SLOT = UNIT_COLUMNS * 2
 
 LOADS = ((0,), (1,), (2,), (3,), (4, 5), (6, 7))
@@ -62,20 +64,31 @@ def tile_nonlocalnd_bn_pa_t_kernel(
 
         vectors = (k_var, k_gamma, bk, k_mean, k_beta, bv)
         VAR, GAMMA, BK, MEAN, BETA, BV = range(6)
-        vector_raw = const.tile([P, len(vectors), 2 * OUT_TILES], BF16)
+        identity = const.tile([P, P], BF16)
+        make_identity(nc, identity[:])
+        vector_rows = const.tile([P, OUT_CHANNELS], BF16, align_bytes=256)
+        vector_raw = const.tile([P, len(vectors), OUT_TILES], F32)
         std = const.tile([P, OUT_TILES], F32)
 
         def load_vectors():
             for v, vector in enumerate(vectors):
-                nc.scalar.dma_start(
-                    out=vector_raw[:, v, :OUT_TILES],
-                    in_=vector.rearrange("(p j) -> p j", p=P),
+                nc.sync.dma_start(
+                    out=vector_rows[ROW_STEP * v : ROW_STEP * v + 1, :],
+                    in_=vector.rearrange("(o n) -> o n", o=1),
                 )
-            nc.scalar.activation(out=std[:], in_=vector_raw[:, VAR, :OUT_TILES], func=SQRT, bias=EPS)
+            acc = psum.tile([P, OUT_TILES, P], BF16)
+            for j in range(OUT_TILES):
+                nc.tensor.transpose(acc[:, j, :], vector_rows[:, j:OUT_CHANNELS:OUT_TILES], identity[:])
+            nc.scalar.copy(
+                out=vector_raw[:],
+                in_=acc[:, :, 0 : ROW_STEP * len(vectors) : ROW_STEP].rearrange("p j v -> p v j"),
+            )
+            nc.scalar.activation(out=std[:], in_=vector_raw[:, VAR, :], func=SQRT, bias=EPS)
 
         raw_words = const.tile([P, CONVS, PASSES, 2 * OUT_CHANNELS], U8, align_bytes=64)
         raw_scales = const.tile([P, CONVS, PASSES, OUT_CHANNELS], U8, align_bytes=64)
         nc.vector.memset(raw_scales[:].bitcast(I32), 0)
+        nc.vector.memset(vector_rows[:], 0.0)
         x_units = []
 
         def load_units(units):
@@ -148,12 +161,12 @@ def tile_nonlocalnd_bn_pa_t_kernel(
             row_maxes[u] = row_max
 
         def max_columns(u):
-            col_pairs = row_maxes[u][:].rearrange("p (t n two) -> p n t two", t=PACK, two=2)
+            col_pairs = row_maxes[u][:].rearrange("p (t c i two) -> p c t i two", t=PACK, i=4, two=2)
             grouped = work.tile([P, PIXELS * PACK], BF16, align_bytes=64)
             nc.vector.tensor_max(
-                out=grouped[:].rearrange("p (n t) -> p n t", t=PACK),
-                in0=col_pairs[:, :, :, 0],
-                in1=col_pairs[:, :, :, 1],
+                out=grouped[:].rearrange("p (c i t) -> p c t i", t=PACK, i=4),
+                in0=col_pairs[:, :, :, :, 0],
+                in1=col_pairs[:, :, :, :, 1],
             )
             groupeds[u] = grouped
 
@@ -175,7 +188,7 @@ def tile_nonlocalnd_bn_pa_t_kernel(
         centred_scaled = const.tile([P, OUT_TILES], F32)
 
         def column(v):
-            return vector_raw[:, v, :OUT_TILES]
+            return vector_raw[:, v, :]
 
         small_work = [
             lambda: nc.vector.reciprocal(out=inv_std[:], in_=std[:]),
@@ -275,7 +288,7 @@ def tile_nonlocalnd_bn_pa_t_kernel(
                     next_small()
             if s < UNITS:
                 max_rows(s)
-                if s >= 1:
+                if s >= 2:
                     next_small()
             if s == 0:
                 reorder_scales(0)

from contextlib import ExitStack

import concourse.mybir as mybir
from concourse.masks import make_identity

BF16 = mybir.dt.bfloat16
F32 = mybir.dt.float32
I32 = mybir.dt.int32
U32 = mybir.dt.uint32
U8 = mybir.dt.uint8
FP8X4 = mybir.dt.float8_e4m3fn_x4
FP4X4 = mybir.dt.float4_e2m1fn_x4
IDENTITY = mybir.ActivationFunctionType.Identity
SQRT = mybir.ActivationFunctionType.Sqrt
MULT = mybir.AluOpType.mult
ADD = mybir.AluOpType.add

BATCH, CHANNELS, HEIGHT, WIDTH, OUT_CHANNELS = 4, 1024, 64, 32, 1024
EPS = 1e-5
PIXELS = (HEIGHT // 2) * (WIDTH // 2)

P = 128
PACK = 4
PASSES = CHANNELS // (P * PACK)
OUT_TILES = OUT_CHANNELS // P
CONVS = 2
UNITS = BATCH * PASSES
UNIT_COLUMNS = PACK * HEIGHT * WIDTH
LIVE_ROWS = 4
QUADRANTS = 4
ROW_STEP = 4
SLOT = UNIT_COLUMNS * 2

LOADS = ((0,), (1,), (2,), (3,), (4, 5), (6, 7))
STORES = (
    (1, (0,), 8 * SLOT),
    (0, (0, 1), 0),
    (1, (1,), 9 * SLOT),
    (0, (2,), 2 * SLOT),
    (1, (2,), 3 * SLOT),
    (0, (3,), 4 * SLOT),
    (1, (3,), 5 * SLOT),
)
CONV_ORDER = ((0, 1), (0, 1), (0, 1), (0, 1))

FLOPS = 2 * CONVS * BATCH * OUT_CHANNELS * CHANNELS * PIXELS


def tile_nonlocalnd_bn_pa_t_kernel(
    tc, x, wk_words, wk_scales, bk, wv_words, wv_scales, bv, k_gamma, k_beta, k_mean, k_var, out_0, out_1
):
    nc = tc.nc
    words_in = (wk_words, wv_words)
    scales_in = (wk_scales, wv_scales)
    outs = (out_0, out_1)

    with ExitStack() as stack:
        stack.enter_context(tc.manual_schedule())
        const = stack.enter_context(tc.tile_pool(name="const", bufs=1))
        region = stack.enter_context(tc.tile_pool(name="region", bufs=1))
        work = stack.enter_context(tc.tile_pool(name="work", bufs=2))
        quant = stack.enter_context(tc.tile_pool(name="quant", bufs=BATCH))
        psum = stack.enter_context(tc.psum_pool(name="psum", bufs=8))

        vectors = (k_var, k_gamma, bk, k_mean, k_beta, bv)
        VAR, GAMMA, BK, MEAN, BETA, BV = range(6)
        identity = const.tile([P, P], BF16)
        make_identity(nc, identity[:])
        vector_rows = const.tile([P, OUT_CHANNELS], BF16, align_bytes=256)
        vector_raw = const.tile([P, len(vectors), OUT_TILES], F32)
        std = const.tile([P, OUT_TILES], F32)

        def load_vectors():
            for v, vector in enumerate(vectors):
                nc.sync.dma_start(
                    out=vector_rows[ROW_STEP * v : ROW_STEP * v + 1, :],
                    in_=vector.rearrange("(o n) -> o n", o=1),
                )
            acc = psum.tile([P, OUT_TILES, P], BF16)
            for j in range(OUT_TILES):
                nc.tensor.transpose(acc[:, j, :], vector_rows[:, j:OUT_CHANNELS:OUT_TILES], identity[:])
            nc.scalar.copy(
                out=vector_raw[:],
                in_=acc[:, :, 0 : ROW_STEP * len(vectors) : ROW_STEP].rearrange("p j v -> p v j"),
            )
            nc.scalar.activation(out=std[:], in_=vector_raw[:, VAR, :], func=SQRT, bias=EPS)

        raw_words = const.tile([P, CONVS, PASSES, 2 * OUT_CHANNELS], U8, align_bytes=64)
        raw_scales = const.tile([P, CONVS, PASSES, OUT_CHANNELS], U8, align_bytes=64)
        nc.vector.memset(raw_scales[:].bitcast(I32), 0)
        nc.vector.memset(vector_rows[:], 0.0)
        x_units = []

        def load_units(units):
            b, c = divmod(units[0], PASSES)
            x_tile = region.tile(
                [P, len(units), UNIT_COLUMNS], BF16, name="x_tile%d" % units[0], offset=units[0] * SLOT
            )
            nc.sync.dma_start(
                out=x_tile[:],
                in_=x[b].rearrange("(c p t) h w -> p c (t h w)", p=P, t=PACK)[:, c : c + len(units), :],
            )
            for i in range(len(units)):
                x_units.append(x_tile[:, i, :])

        def load_words(conv):
            nc.sync.dma_start(
                out=raw_words[:, conv, :, :].bitcast(I32),
                in_=words_in[conv].bitcast(I32).rearrange("c p n -> p c n"),
            )

        def load_scales(conv):
            rows = scales_in[conv].bitcast(I32).rearrange("c q n -> q c n")
            for quadrant in range(QUADRANTS):
                nc.sync.dma_start(
                    out=raw_scales[32 * quadrant : 32 * quadrant + LIVE_ROWS, conv, :, :].bitcast(I32),
                    in_=rows[LIVE_ROWS * quadrant : LIVE_ROWS * (quadrant + 1)],
                )

        load_words(0)
        load_words(1)
        load_units(LOADS[0])
        load_scales(0)
        load_units(LOADS[1])
        load_vectors()
        load_units(LOADS[2])
        load_units(LOADS[3])
        load_scales(1)
        for units in LOADS[4:]:
            load_units(units)

        w_words = const.tile([P, CONVS, PASSES, 2 * OUT_CHANNELS], U8, align_bytes=64)
        w_scales = const.tile([P, CONVS, PASSES, OUT_CHANNELS], U8, align_bytes=64)

        def reorder_words(conv):
            for c in range(PASSES):
                nc.vector.tensor_copy(
                    out=w_words[:, conv, c, :].rearrange("p (j m two) -> p j m two", j=OUT_TILES, two=2),
                    in_=raw_words[:, conv, c, :].rearrange("p (m j two) -> p j m two", j=OUT_TILES, two=2),
                )

        def reorder_scales(conv):
            nc.vector.tensor_copy(
                out=w_scales[:, conv, :, :].rearrange("p c (j m) -> p c j m", j=OUT_TILES),
                in_=raw_scales[:, conv, :, :].rearrange("p c (m j) -> p c j m", j=OUT_TILES),
            )

        x_codes = []
        x_scales = []
        row_maxes = {}
        groupeds = {}

        def max_rows(u):
            row_pairs = x_units[u].rearrange("p (r two w) -> p r two w", two=2, w=WIDTH)
            row_max = work.tile([P, PACK * PIXELS * 2], BF16)
            nc.vector.tensor_max(
                out=row_max[:].rearrange("p (r w) -> p r w", w=WIDTH),
                in0=row_pairs[:, :, 0, :],
                in1=row_pairs[:, :, 1, :],
            )
            row_maxes[u] = row_max

        def max_columns(u):
            col_pairs = row_maxes[u][:].rearrange("p (t c i two) -> p c t i two", t=PACK, i=4, two=2)
            grouped = work.tile([P, PIXELS * PACK], BF16, align_bytes=64)
            nc.vector.tensor_max(
                out=grouped[:].rearrange("p (c i t) -> p c t i", t=PACK, i=4),
                in0=col_pairs[:, :, :, :, 0],
                in1=col_pairs[:, :, :, :, 1],
            )
            groupeds[u] = grouped

        def quantise(u):
            b, c = divmod(u, PASSES)
            if c == 0:
                codes = quant.tile([P, PASSES, PIXELS], U32, align_bytes=64)
                planes = quant.tile([P, PASSES, PIXELS], U8, align_bytes=64)
                x_codes.append(codes)
                x_scales.append(planes)
            nc.vector.quantize_mx(
                out=x_codes[b][:, c, :].bitcast(FP8X4), scales=x_scales[b][:, c, :], in_=groupeds[u][:]
            )

        scale = const.tile([P, CONVS, OUT_TILES], F32)
        shift = const.tile([P, CONVS, OUT_TILES], F32)
        inv_std = const.tile([P, OUT_TILES], F32)
        centred = const.tile([P, OUT_TILES], F32)
        centred_scaled = const.tile([P, OUT_TILES], F32)

        def column(v):
            return vector_raw[:, v, :]

        small_work = [
            lambda: nc.vector.reciprocal(out=inv_std[:], in_=std[:]),
            lambda: nc.vector.tensor_sub(out=centred[:], in0=column(BK), in1=column(MEAN)),
            lambda: nc.vector.tensor_mul(out=scale[:, 0, :], in0=column(GAMMA), in1=inv_std[:]),
            lambda: nc.vector.memset(scale[:, 1, :], 1.0),
            lambda: nc.vector.tensor_mul(out=centred_scaled[:], in0=centred[:], in1=scale[:, 0, :]),
            lambda: nc.vector.tensor_copy(out=shift[:, 1, :], in_=column(BV)),
            lambda: nc.vector.tensor_add(out=shift[:, 0, :], in0=centred_scaled[:], in1=column(BETA)),
        ]
        small_done = []

        def next_small():
            for repeat in range(2):
                if len(small_done) < len(small_work):
                    small_work[len(small_done)]()
                    small_done.append(True)

        def multiply(acc, b, conv, j, c):
            nc.tensor.matmul_mx(
                out=acc[:],
                lhsT=w_words[:, conv, c, 2 * P * j : 2 * P * (j + 1)].bitcast(FP4X4),
                lhsT_scale=w_scales[:, conv, c, P * j : P * (j + 1)],
                rhs=x_codes[b][:, c, :].bitcast(FP8X4),
                rhs_scale=x_scales[b][:, c, :],
                start=(c == 0),
                stop=(c == PASSES - 1),
            )

        opened = []

        def open_first(b):
            for j in range(OUT_TILES):
                acc = psum.tile([P, PIXELS], F32)
                multiply(acc, b, CONV_ORDER[b][0], j, 0)
                opened.append(acc)

        staged_tiles = {}

        def staged_for(conv, b):
            for i, (store_conv, images, offset) in enumerate(STORES):
                if store_conv == conv and b in images:
                    if i not in staged_tiles:
                        staged = region.tile(
                            [P, len(images), OUT_TILES, PIXELS], F32, name="staged%d" % i, offset=offset
                        )
                        staged_tiles[i] = staged
                    return staged_tiles[i], images, images.index(b)
            raise ValueError("no store")

        def convolve(b, vector_helps):
            for turn, conv in enumerate(CONV_ORDER[b]):
                staged, images, place = staged_for(conv, b)
                for j in range(OUT_TILES):
                    if turn == 0:
                        acc = opened[OUT_TILES * b + j]
                    else:
                        acc = psum.tile([P, PIXELS], F32)
                        multiply(acc, b, conv, j, 0)
                    multiply(acc, b, conv, j, 1)
                    if vector_helps and j % 2 == 1:
                        nc.vector.tensor_scalar(
                            out=staged[:, place, j, :],
                            in0=acc[:],
                            scalar1=scale[:, conv, j : j + 1],
                            scalar2=shift[:, conv, j : j + 1],
                            op0=MULT,
                            op1=ADD,
                        )
                    else:
                        nc.scalar.activation(
                            out=staged[:, place, j, :],
                            in_=acc[:],
                            func=IDENTITY,
                            bias=shift[:, conv, j : j + 1],
                            scale=scale[:, conv, j : j + 1],
                        )
                if b == images[-1]:
                    nc.sync.dma_start(
                        out=outs[conv][images[0] : images[-1] + 1].rearrange(
                            "b (p j) r w -> p b (j r w)", p=P
                        ),
                        in_=staged[:].rearrange("p b j n -> p b (j n)"),
                    )

        reorder_words(0)
        reorder_words(1)
        for s in range(UNITS + 2):
            if 0 <= s - 2:
                quantise(s - 2)
                next_small()
            if s == 3:
                reorder_scales(1)
            if 0 <= s - 1 < UNITS:
                max_columns(s - 1)
                if s >= 2:
                    next_small()
            if s < UNITS:
                max_rows(s)
                if s >= 2:
                    next_small()
            if s == 0:
                reorder_scales(0)
            if s >= 2 and s % 2 == 0:
                open_first((s - 2) // 2)
            if s >= 3 and s % 2 == 1:
                b = (s - 3) // 2
                convolve(b, vector_helps=(b == BATCH - 1))
